import numpy as np
import ml_dtypes


def mxq(x, axis, fmt="e4m3"):
    dtype, down = {"e4m3": (ml_dtypes.float8_e4m3fn, 7), "e5m2": (ml_dtypes.float8_e5m2, 14)}[fmt]
    v = np.moveaxis(np.asarray(x, np.float32).astype(ml_dtypes.bfloat16).astype(np.float64), axis, -1)
    blocks = v.reshape(v.shape[:-1] + (-1, 32))
    amax = np.abs(blocks).max(-1, keepdims=True)
    byte = np.maximum(np.where(amax > 0, np.frexp(amax)[1] - 1 + 127, 0) - down, 1)
    scale = np.exp2(byte - 127.0)
    codes = (blocks / scale).astype(np.float32).astype(dtype).astype(np.float64)
    return np.moveaxis((codes * scale).reshape(v.shape), -1, axis)


WIDE = False


def mx_kscale(k):
    if not WIDE:
        return np.ones(k)
    levels = np.array([10, -10, 5, -5, 0])
    a = np.random.permutation(np.resize(levels, k // 512 * 4)).reshape(k // 512, 4)
    idx = np.arange(k)
    return np.exp2(a[idx // 512, idx % 128 // 32])


BF16 = ml_dtypes.bfloat16


def bf(x):
    return np.asarray(x, np.float32).astype(BF16)


def f64(x):
    return np.asarray(x).astype(np.float64)


E2M1 = np.array([0.0, 0.5, 1.0, 1.5, 2.0, 3.0, 4.0, 6.0, -0.0, -0.5, -1.0, -1.5, -2.0, -3.0, -4.0, -6.0])


def pack_weight(w, fmt):
    k, n = w.shape
    w = f64(bf(w)).reshape(k // 32, 32, n)
    amax = np.abs(w).max(1)
    if fmt == "e4m3":
        byte = np.frexp(amax)[1] - 1 + 127 - 7
    else:
        mant, ex = np.frexp(amax / 6.0)
        byte = np.where(mant > 0.5, ex, ex - 1) + 127
    byte = np.clip(np.where(amax > 0, byte, 1), 1, 254)
    scaled = (w * np.exp2(127.0 - byte)[:, None, :]).reshape(k, n).astype(np.float32)
    by_word = np.ascontiguousarray(scaled.reshape(k // 512, 128, 4, n).transpose(0, 1, 3, 2))
    if fmt == "e4m3":
        words = by_word.astype(ml_dtypes.float8_e4m3fn).view(np.uint8)
    else:
        c = by_word.astype(ml_dtypes.float4_e2m1fn).view(np.uint8) & 0xF
        words = c[..., 0::2] | (c[..., 1::2] << 4)
    return np.ascontiguousarray(words), np.ascontiguousarray(byte.astype(np.uint8).reshape(k // 512, 16, n))


def unpack_weight(words, scales, fmt):
    g, p, n, _ = words.shape
    if fmt == "e4m3":
        vals = np.ascontiguousarray(words).view(ml_dtypes.float8_e4m3fn).astype(np.float64)
    else:
        nib = np.empty((g, p, n, 4), np.uint8)
        nib[..., 0::2] = words & 0xF
        nib[..., 1::2] = words >> 4
        vals = E2M1[nib]
    vals = vals * np.repeat(np.exp2(scales.astype(np.float64) - 127.0), 8, axis=1)[..., None]
    return vals.transpose(0, 1, 3, 2).reshape(g * 512, n)


B, T, C, NH, KV, HD, W = 2, 64, 8192, 16, 4, 128, 256
G = NH // KV
ROPE_THETA = 10000.0
QK_RMS = 2.0
FMT = "e4m3"


def sine_table():
    fraction = np.arange(0, HD, 2) / HD
    inv_timescale = 1.0 / ROPE_THETA ** fraction
    sinusoid = np.arange(T)[:, None] * inv_timescale[None, :]
    sinusoid = np.concatenate([sinusoid, sinusoid], axis=-1)
    return np.sin(sinusoid), np.cos(sinusoid)


def rotate_half(u):
    u1, u2 = np.split(u, 2, axis=-1)
    return np.concatenate([-u2, u1], axis=-1)


def setup_inputs():
    s = mx_kscale(C)
    x = bf(np.random.standard_normal((B, T, C)) * s)
    q_words, q_scales = pack_weight(np.random.standard_normal((C, NH * HD)) * QK_RMS / np.sqrt(C) / s[:, None], FMT)
    k_words, k_scales = pack_weight(np.random.standard_normal((C, KV * HD)) * QK_RMS / np.sqrt(C) / s[:, None], FMT)
    v_words, v_scales = pack_weight(np.random.standard_normal((C, KV * HD)) / np.sqrt(C) / s[:, None], FMT)
    return {"x": x,
            "q_kernel_words": q_words, "q_kernel_scales": q_scales,
            "k_kernel_words": k_words, "k_kernel_scales": k_scales,
            "v_kernel_words": v_words, "v_kernel_scales": v_scales}


def reference(x, q_kernel_words, q_kernel_scales, k_kernel_words, k_kernel_scales, v_kernel_words, v_kernel_scales):
    xq = mxq(f64(x), 2, "e4m3")
    q = (xq @ unpack_weight(q_kernel_words, q_kernel_scales, FMT)).reshape(B, T, KV, G, HD)
    k = (xq @ unpack_weight(k_kernel_words, k_kernel_scales, FMT)).reshape(B, T, KV, HD)
    v = (xq @ unpack_weight(v_kernel_words, v_kernel_scales, FMT)).reshape(B, T, KV, HD)
    sin, cos = sine_table()
    q = q * cos[None, :, None, None, :] + rotate_half(q) * sin[None, :, None, None, :]
    k = k * cos[None, :, None, :] + rotate_half(k) * sin[None, :, None, :]
    return q * HD ** (-0.5), k, v

@@ -1,0 +1,280 @@
+import math
+from contextlib import ExitStack
+
+import concourse.mybir as mybir
+from concourse.masks import make_identity
+
+F32 = mybir.dt.float32
+BF16 = mybir.dt.bfloat16
+I32 = mybir.dt.int32
+U32 = mybir.dt.uint32
+U8 = mybir.dt.uint8
+FP8X4 = mybir.dt.float8_e4m3fn_x4
+ALU = mybir.AluOpType
+ACT = mybir.ActivationFunctionType
+
+P = 128
+PACK = 4
+K_PASS = P * PACK
+C = 8192
+GROUPS = C // K_PASS
+POSITIONS = 64
+HEAD_DIM = 128
+HALF = HEAD_DIM // 2
+BANK = 512
+HEADS_PER_BANK = BANK // HEAD_DIM
+Q_COLS = 2048
+KV_COLS = 512
+ALL_COLS = Q_COLS + 2 * KV_COLS
+K_START = Q_COLS
+V_START = Q_COLS + KV_COLS
+
+PLANES_TOGETHER = 4
+ROUNDS = GROUPS // PLANES_TOGETHER
+QUADRANTS = 4
+ROWS_PER_QUADRANT = 4
+
+X_CHUNK_GROUPS = 4
+X_CHUNKS = GROUPS // X_CHUNK_GROUPS
+WORDS_PER_GROUP = K_PASS // 2
+
+ROPE_THETA = 10000.0
+FREQ_RATIO = ROPE_THETA ** (-1.0 / HALF)
+TWO_PI = 2.0 * math.pi
+TWO_PI_HIGH = 6.28125
+TWO_PI_LOW = TWO_PI - TWO_PI_HIGH
+ROUND_MAGIC = 1.5 * 2.0**23
+
+FLOPS = 2 * P * C * ALL_COLS
+
+
+def tile_attention_pa_k_kernel(
+    tc,
+    x,
+    q_kernel_words,
+    q_kernel_scales,
+    k_kernel_words,
+    k_kernel_scales,
+    v_kernel_words,
+    v_kernel_scales,
+    out_0,
+    out_1,
+    out_2,
+):
+    nc = tc.nc
+    with ExitStack() as ctx:
+        keep = ctx.enter_context(tc.tile_pool(name="keep", bufs=1))
+        weights = ctx.enter_context(tc.tile_pool(name="weights", bufs=GROUPS))
+        stage = ctx.enter_context(tc.tile_pool(name="stage", bufs=2))
+        psum_x = ctx.enter_context(tc.psum_pool(name="psum_x", bufs=2))
+        psum_acc = ctx.enter_context(tc.psum_pool(name="psum_acc", bufs=1))
+        ctx.enter_context(tc.manual_schedule())
+
+        def words_of_group(words, g):
+            return words[g].rearrange("p n t -> p (n t)").bitcast(I32)
+
+        x_rows = x.rearrange("b t c -> (b t) c")
+        x_sb = keep.tile([P, C], BF16, name="x_sb")
+        for chunk in range(X_CHUNKS):
+            cols = slice(chunk * X_CHUNK_GROUPS * K_PASS, (chunk + 1) * X_CHUNK_GROUPS * K_PASS)
+            nc.sync.dma_start(out=x_sb[:, cols], in_=x_rows[:, cols])
+        q_words = []
+        for g in range(GROUPS):
+            tile_q = weights.tile([P, Q_COLS], U32, name="tile_q", tag="words", align_bytes=64)
+            nc.sync.dma_start(out=tile_q[:].bitcast(I32), in_=words_of_group(q_kernel_words, g))
+            q_words.append(tile_q)
+
+        identity = keep.tile([P, P], F32, name="identity")
+        make_identity(nc, identity[:])
+        row_number = keep.tile([P, 1], I32, name="row_number")
+        nc.gpsimd.iota(row_number[:], pattern=[[0, 1]], base=0, channel_multiplier=1)
+
+        planes = keep.tile([P, ROUNDS, ALL_COLS], U8, name="planes", align_bytes=64)
+        for a in range(ROUNDS):
+            nc.vector.memset(planes[:, a, :].bitcast(I32), 0)
+
+        def load_planes(scales, start, width):
+            for a in range(ROUNDS):
+                for quadrant in range(QUADRANTS):
+                    first = 32 * quadrant
+                    nc.gpsimd.dma_start(
+                        out=planes[first : first + 16, a, start : start + width].bitcast(F32),
+                        in_=scales[
+                            PLANES_TOGETHER * a : PLANES_TOGETHER * (a + 1),
+                            ROWS_PER_QUADRANT * quadrant : ROWS_PER_QUADRANT * (quadrant + 1),
+                            :,
+                        ].bitcast(F32),
+                    )
+
+        load_planes(q_kernel_scales, 0, Q_COLS)
+        load_planes(k_kernel_scales, K_START, KV_COLS)
+        load_planes(v_kernel_scales, V_START, KV_COLS)
+
+        x_pairs = x_sb[:].bitcast(F32)
+        x_codes = keep.tile([P, GROUPS * P], U32, name="x_codes", align_bytes=64)
+        x_scales = keep.tile([P, GROUPS * P], U8, name="x_scales", align_bytes=64)
+        for chunk in range(X_CHUNKS):
+            grouped = stage.tile([P, X_CHUNK_GROUPS, P, PACK], BF16, name="grouped", align_bytes=64)
+            for pair in range(X_CHUNK_GROUPS // 2):
+                turned = psum_x.tile([P, 2, 2, P], F32, name="turned")
+                for i in range(2):
+                    first = (chunk * X_CHUNK_GROUPS + 2 * pair + i) * WORDS_PER_GROUP
+                    for u in range(2):
+                        nc.tensor.transpose(
+                            turned[:, i, u, :],
+                            x_pairs[:, first + u : first + WORDS_PER_GROUP : 2],
+                            identity[:],
+                        )
+                nc.scalar.copy(
+                    out=grouped[:, 2 * pair : 2 * pair + 2, :, :].bitcast(F32),
+                    in_=turned[:].rearrange("p i u r -> p i r u"),
+                )
+            cols = slice(chunk * X_CHUNK_GROUPS * P, (chunk + 1) * X_CHUNK_GROUPS * P)
+            nc.vector.quantize_mx(
+                out=x_codes[:, cols].bitcast(FP8X4),
+                scales=x_scales[:, cols],
+                in_=grouped[:].rearrange("p g r t -> p (g r t)"),
+            )
+
+        position_int = keep.tile([P, 1], I32, name="position_int")
+        nc.vector.tensor_scalar(
+            out=position_int[:], in0=row_number[:], scalar1=POSITIONS - 1, scalar2=None, op0=ALU.bitwise_and
+        )
+        position = keep.tile([P, 1], F32, name="position")
+        nc.vector.tensor_copy(out=position[:], in_=position_int[:])
+        inv_freq = keep.tile([P, HALF], F32, name="inv_freq")
+        nc.vector.memset(inv_freq[:, 0:1], 1.0)
+        for doubling in range(6):
+            done = 1 << doubling
+            nc.vector.tensor_scalar(
+                out=inv_freq[:, done : 2 * done],
+                in0=inv_freq[:, 0:done],
+                scalar1=FREQ_RATIO**done,
+                scalar2=None,
+                op0=ALU.mult,
+            )
+        angle = keep.tile([P, 2, HALF], F32, name="angle")
+        nc.vector.tensor_scalar(
+            out=angle[:, 0, :], in0=inv_freq[:], scalar1=position[:, 0:1], scalar2=None, op0=ALU.mult
+        )
+        nc.vector.tensor_scalar(
+            out=angle[:, 1, :],
+            in0=inv_freq[:],
+            scalar1=position[:, 0:1],
+            scalar2=math.pi / 2.0,
+            op0=ALU.mult,
+            op1=ALU.add,
+        )
+        turns = keep.tile([P, 2, HALF], F32, name="turns")
+        nc.vector.tensor_scalar(
+            out=turns[:], in0=angle[:], scalar1=1.0 / TWO_PI, scalar2=ROUND_MAGIC, op0=ALU.mult, op1=ALU.add
+        )
+        nc.vector.tensor_scalar(out=turns[:], in0=turns[:], scalar1=ROUND_MAGIC, scalar2=None, op0=ALU.subtract)
+        reduced = keep.tile([P, 2, HALF], F32, name="reduced")
+        nc.vector.scalar_tensor_tensor(
+            out=reduced[:], in0=turns[:], scalar=-TWO_PI_HIGH, in1=angle[:], op0=ALU.mult, op1=ALU.add
+        )
+        nc.vector.scalar_tensor_tensor(
+            out=reduced[:], in0=turns[:], scalar=-TWO_PI_LOW, in1=reduced[:], op0=ALU.mult, op1=ALU.add
+        )
+        sin_cos = keep.tile([P, 2, HALF], F32, name="sin_cos")
+        nc.scalar.activation(out=sin_cos[:], in_=reduced[:], func=ACT.Sin)
+
+        def rotation_tables(factor, label):
+            cos_tab = keep.tile([P, 2, HALF], F32, name="cos_" + label)
+            sin_tab = keep.tile([P, 2, HALF], F32, name="sin_" + label)
+            nc.vector.tensor_scalar(
+                out=cos_tab[:],
+                in0=sin_cos[:, 1:2, :].to_broadcast([P, 2, HALF]),
+                scalar1=factor,
+                scalar2=None,
+                op0=ALU.mult,
+            )
+            nc.vector.tensor_scalar(
+                out=sin_tab[:, 0, :], in0=sin_cos[:, 0, :], scalar1=factor, scalar2=None, op0=ALU.mult
+            )
+            nc.vector.tensor_scalar(
+                out=sin_tab[:, 1, :], in0=sin_cos[:, 0, :], scalar1=-factor, scalar2=None, op0=ALU.mult
+            )
+            return cos_tab, sin_tab
+
+        q_tables = rotation_tables(HEAD_DIM**-0.5, "q")
+        k_tables = rotation_tables(1.0, "k")
+
+        def mx_pass(acc, g, words, plane_start):
+            a, j = divmod(g, PLANES_TOGETHER)
+            tokens = slice(g * P, (g + 1) * P)
+            nc.tensor.matmul_mx(
+                out=acc[:],
+                lhsT=x_codes[:, tokens].bitcast(FP8X4),
+                lhsT_scale=x_scales[:, tokens],
+                rhs=words.bitcast(FP8X4),
+                rhs_scale=planes[ROWS_PER_QUADRANT * j : P, a, plane_start : plane_start + BANK],
+                start=(g == 0),
+                stop=(g == GROUPS - 1),
+            )
+
+        def rotate_and_store(acc, tables, dest):
+            cos_tab, sin_tab = tables
+            heads = acc[:].rearrange("p (h d) -> p h d", d=HEAD_DIM)
+            shape = [P, HEADS_PER_BANK, HEAD_DIM]
+            by_cos = stage.tile([P, HEADS_PER_BANK, 2, HALF], F32, name="by_cos")
+            by_sin = stage.tile([P, HEADS_PER_BANK, 2, HALF], F32, name="by_sin")
+            rotated = stage.tile([P, HEADS_PER_BANK, 2, HALF], F32, name="rotated")
+            nc.vector.tensor_tensor(
+                out=by_cos[:].rearrange("p h s f -> p h (s f)"),
+                in0=heads,
+                in1=cos_tab[:].rearrange("p s f -> p (s f)").unsqueeze(1).to_broadcast(shape),
+                op=ALU.mult,
+            )
+            nc.vector.tensor_tensor(
+                out=by_sin[:].rearrange("p h s f -> p h (s f)"),
+                in0=heads,
+                in1=sin_tab[:].rearrange("p s f -> p (s f)").unsqueeze(1).to_broadcast(shape),
+                op=ALU.mult,
+            )
+            for half in range(2):
+                nc.vector.tensor_tensor(
+                    out=rotated[:, :, half, :],
+                    in0=by_cos[:, :, half, :],
+                    in1=by_sin[:, :, 1 - half, :],
+                    op=ALU.add,
+                )
+            nc.scalar.dma_start(out=dest, in_=rotated[:].rearrange("p h s f -> p (h s f)"))
+
+        q_banks = Q_COLS // BANK
+        acc_q = [psum_acc.tile([P, BANK], F32, name="acc_q%d" % bank) for bank in range(q_banks)]
+        for g in range(GROUPS):
+            for bank in range(q_banks):
+                mx_pass(acc_q[bank], g, q_words[g][:, bank * BANK : (bank + 1) * BANK], bank * BANK)
+
+        kv_words = []
+        for words in (k_kernel_words, v_kernel_words):
+            for a in range(ROUNDS):
+                tile_kv = weights.tile(
+                    [P, PLANES_TOGETHER, KV_COLS], U32, name="tile_kv", tag="words", align_bytes=64
+                )
+                for j in range(PLANES_TOGETHER):
+                    nc.sync.dma_start(
+                        out=tile_kv[:, j, :].bitcast(I32),
+                        in_=words_of_group(words, PLANES_TOGETHER * a + j),
+                    )
+                kv_words.append(tile_kv)
+
+        q_out = out_0.rearrange("b t k g d -> (b t) (k g d)")
+        for bank in range(q_banks):
+            rotate_and_store(acc_q[bank], q_tables, q_out[:, bank * BANK : (bank + 1) * BANK])
+
+        acc_k = psum_acc.tile([P, BANK], F32, name="acc_k")
+        for g in range(GROUPS):
+            a, j = divmod(g, PLANES_TOGETHER)
+            mx_pass(acc_k, g, kv_words[a][:, j, :], K_START)
+        rotate_and_store(acc_k, k_tables, out_1.rearrange("b t k d -> (b t) (k d)"))
+
+        acc_v = psum_acc.tile([P, BANK], F32, name="acc_v")
+        for g in range(GROUPS):
+            a, j = divmod(g, PLANES_TOGETHER)
+            mx_pass(acc_v, g, kv_words[ROUNDS + a][:, j, :], V_START)
+        v_sb = stage.tile([P, BANK], F32, name="v_sb")
+        nc.vector.tensor_copy(out=v_sb[:], in_=acc_v[:])
+        nc.sync.dma_start(out=out_2.rearrange("b t k d -> (b t) (k d)"), in_=v_sb[:])

@@ -26,8 +26,6 @@ HEADS_PER_BANK = BANK // HEAD_DIM
 Q_COLS = 2048
 KV_COLS = 512
 ALL_COLS = Q_COLS + 2 * KV_COLS
-K_START = Q_COLS
-V_START = Q_COLS + KV_COLS
 
 PLANES_TOGETHER = 4
 ROUNDS = GROUPS // PLANES_TOGETHER
@@ -66,6 +64,7 @@ def tile_attention_pa_k_kernel(
         keep = ctx.enter_context(tc.tile_pool(name="keep", bufs=1))
         weights = ctx.enter_context(tc.tile_pool(name="weights", bufs=GROUPS))
         stage = ctx.enter_context(tc.tile_pool(name="stage", bufs=2))
+        results = ctx.enter_context(tc.tile_pool(name="results", bufs=Q_COLS // BANK + 1))
         psum_x = ctx.enter_context(tc.psum_pool(name="psum_x", bufs=2))
         psum_acc = ctx.enter_context(tc.psum_pool(name="psum_acc", bufs=1))
         ctx.enter_context(tc.manual_schedule())
@@ -89,26 +88,22 @@ def tile_attention_pa_k_kernel(
         row_number = keep.tile([P, 1], I32, name="row_number")
         nc.gpsimd.iota(row_number[:], pattern=[[0, 1]], base=0, channel_multiplier=1)
 
-        planes = keep.tile([P, ROUNDS, ALL_COLS], U8, name="planes", align_bytes=64)
-        for a in range(ROUNDS):
-            nc.vector.memset(planes[:, a, :].bitcast(I32), 0)
-
-        def load_planes(scales, start, width):
-            for a in range(ROUNDS):
-                for quadrant in range(QUADRANTS):
-                    first = 32 * quadrant
+        def load_planes(scales, width, label):
+            planes = keep.tile([P, ROUNDS, width], U8, name="planes_" + label, align_bytes=64)
+            nc.vector.memset(planes[:].bitcast(I32), 0)
+            by_plane = scales.rearrange("(a j) q n -> j a q n", j=PLANES_TOGETHER)
+            for quadrant in range(QUADRANTS):
+                for r in range(ROWS_PER_QUADRANT):
+                    first = 32 * quadrant + r
                     nc.gpsimd.dma_start(
-                        out=planes[first : first + 16, a, start : start + width].bitcast(F32),
-                        in_=scales[
-                            PLANES_TOGETHER * a : PLANES_TOGETHER * (a + 1),
-                            ROWS_PER_QUADRANT * quadrant : ROWS_PER_QUADRANT * (quadrant + 1),
-                            :,
-                        ].bitcast(F32),
+                        out=planes[first : 32 * quadrant + 16 : ROWS_PER_QUADRANT, :, :].bitcast(F32),
+                        in_=by_plane[:, :, ROWS_PER_QUADRANT * quadrant + r, :].bitcast(F32),
                     )
+            return planes
 
-        load_planes(q_kernel_scales, 0, Q_COLS)
-        load_planes(k_kernel_scales, K_START, KV_COLS)
-        load_planes(v_kernel_scales, V_START, KV_COLS)
+        q_planes = load_planes(q_kernel_scales, Q_COLS, "q")
+        k_planes = load_planes(k_kernel_scales, KV_COLS, "k")
+        v_planes = load_planes(v_kernel_scales, KV_COLS, "v")
 
         x_pairs = x_sb[:].bitcast(F32)
         x_codes = keep.tile([P, GROUPS * P], U32, name="x_codes", align_bytes=64)
@@ -201,7 +196,7 @@ def tile_attention_pa_k_kernel(
         q_tables = rotation_tables(HEAD_DIM**-0.5, "q")
         k_tables = rotation_tables(1.0, "k")
 
-        def mx_pass(acc, g, words, plane_start):
+        def mx_pass(acc, g, words, planes, plane_start):
             a, j = divmod(g, PLANES_TOGETHER)
             tokens = slice(g * P, (g + 1) * P)
             nc.tensor.matmul_mx(
@@ -220,7 +215,7 @@ def tile_attention_pa_k_kernel(
             shape = [P, HEADS_PER_BANK, HEAD_DIM]
             by_cos = stage.tile([P, HEADS_PER_BANK, 2, HALF], F32, name="by_cos")
             by_sin = stage.tile([P, HEADS_PER_BANK, 2, HALF], F32, name="by_sin")
-            rotated = stage.tile([P, HEADS_PER_BANK, 2, HALF], F32, name="rotated")
+            rotated = results.tile([P, HEADS_PER_BANK, 2, HALF], F32, name="rotated")
             nc.vector.tensor_tensor(
                 out=by_cos[:].rearrange("p h s f -> p h (s f)"),
                 in0=heads,
@@ -240,13 +235,13 @@ def tile_attention_pa_k_kernel(
                     in1=by_sin[:, :, 1 - half, :],
                     op=ALU.add,
                 )
-            nc.scalar.dma_start(out=dest, in_=rotated[:].rearrange("p h s f -> p (h s f)"))
+            nc.sync.dma_start(out=dest, in_=rotated[:].rearrange("p h s f -> p (h s f)"))
 
         q_banks = Q_COLS // BANK
         acc_q = [psum_acc.tile([P, BANK], F32, name="acc_q%d" % bank) for bank in range(q_banks)]
         for g in range(GROUPS):
             for bank in range(q_banks):
-                mx_pass(acc_q[bank], g, q_words[g][:, bank * BANK : (bank + 1) * BANK], bank * BANK)
+                mx_pass(acc_q[bank], g, q_words[g][:, bank * BANK : (bank + 1) * BANK], q_planes, bank * BANK)
 
         kv_words = []
         for words in (k_kernel_words, v_kernel_words):
@@ -268,13 +263,13 @@ def tile_attention_pa_k_kernel(
         acc_k = psum_acc.tile([P, BANK], F32, name="acc_k")
         for g in range(GROUPS):
             a, j = divmod(g, PLANES_TOGETHER)
-            mx_pass(acc_k, g, kv_words[a][:, j, :], K_START)
+            mx_pass(acc_k, g, kv_words[a][:, j, :], k_planes, 0)
         rotate_and_store(acc_k, k_tables, out_1.rearrange("b t k d -> (b t) (k d)"))
 
         acc_v = psum_acc.tile([P, BANK], F32, name="acc_v")
         for g in range(GROUPS):
             a, j = divmod(g, PLANES_TOGETHER)
-            mx_pass(acc_v, g, kv_words[ROUNDS + a][:, j, :], V_START)
+            mx_pass(acc_v, g, kv_words[ROUNDS + a][:, j, :], v_planes, 0)
         v_sb = stage.tile([P, BANK], F32, name="v_sb")
         nc.vector.tensor_copy(out=v_sb[:], in_=acc_v[:])
         nc.sync.dma_start(out=out_2.rearrange("b t k d -> (b t) (k d)"), in_=v_sb[:])

@@ -72,38 +72,56 @@ def tile_attention_pa_k_kernel(
         def words_of_group(words, g):
             return words[g].rearrange("p n t -> p (n t)").bitcast(I32)
 
+        def zeroed_planes(width, label):
+            planes = keep.tile([P, ROUNDS, width], U8, name="planes_" + label, align_bytes=64)
+            nc.vector.memset(planes[:].bitcast(I32), 0)
+            return planes
+
+        q_planes = zeroed_planes(Q_COLS, "q")
+        k_planes = zeroed_planes(KV_COLS, "k")
+        v_planes = zeroed_planes(KV_COLS, "v")
+
+        def load_scale_rows(queue, view, planes, scales, a, quadrant):
+            first = 32 * quadrant
+            queue.dma_start(
+                out=planes[first : first + PLANES_TOGETHER * ROWS_PER_QUADRANT, a, :].bitcast(view),
+                in_=scales[
+                    PLANES_TOGETHER * a : PLANES_TOGETHER * (a + 1),
+                    ROWS_PER_QUADRANT * quadrant : ROWS_PER_QUADRANT * (quadrant + 1),
+                    :,
+                ].bitcast(view),
+            )
+
         x_rows = x.rearrange("b t c -> (b t) c")
         x_sb = keep.tile([P, C], BF16, name="x_sb")
         for chunk in range(X_CHUNKS):
             cols = slice(chunk * X_CHUNK_GROUPS * K_PASS, (chunk + 1) * X_CHUNK_GROUPS * K_PASS)
             nc.sync.dma_start(out=x_sb[:, cols], in_=x_rows[:, cols])
+            for quadrant in range(2):
+                load_scale_rows(nc.sync, I32, q_planes, q_kernel_scales, chunk, quadrant)
         q_words = []
         for g in range(GROUPS):
             tile_q = weights.tile([P, Q_COLS], U32, name="tile_q", tag="words", align_bytes=64)
             nc.sync.dma_start(out=tile_q[:].bitcast(I32), in_=words_of_group(q_kernel_words, g))
             q_words.append(tile_q)
+            a, quadrant = divmod(g % (2 * ROUNDS), 2)
+            if g < 2 * ROUNDS:
+                load_scale_rows(nc.sync, I32, k_planes, k_kernel_scales, a, quadrant)
+            else:
+                load_scale_rows(nc.sync, I32, v_planes, v_kernel_scales, a, quadrant)
 
         identity = keep.tile([P, P], F32, name="identity")
         make_identity(nc, identity[:])
         row_number = keep.tile([P, 1], I32, name="row_number")
         nc.gpsimd.iota(row_number[:], pattern=[[0, 1]], base=0, channel_multiplier=1)
-
-        def load_planes(scales, width, label):
-            planes = keep.tile([P, ROUNDS, width], U8, name="planes_" + label, align_bytes=64)
-            nc.vector.memset(planes[:].bitcast(I32), 0)
-            by_plane = scales.rearrange("(a j) q n -> j a q n", j=PLANES_TOGETHER)
-            for quadrant in range(QUADRANTS):
-                for r in range(ROWS_PER_QUADRANT):
-                    first = 32 * quadrant + r
-                    nc.gpsimd.dma_start(
-                        out=planes[first : 32 * quadrant + 16 : ROWS_PER_QUADRANT, :, :].bitcast(F32),
-                        in_=by_plane[:, :, ROWS_PER_QUADRANT * quadrant + r, :].bitcast(F32),
-                    )
-            return planes
-
-        q_planes = load_planes(q_kernel_scales, Q_COLS, "q")
-        k_planes = load_planes(k_kernel_scales, KV_COLS, "k")
-        v_planes = load_planes(v_kernel_scales, KV_COLS, "v")
+        for planes, scales in (
+            (q_planes, q_kernel_scales),
+            (k_planes, k_kernel_scales),
+            (v_planes, v_kernel_scales),
+        ):
+            for a in range(ROUNDS):
+                for quadrant in range(2, QUADRANTS):
+                    load_scale_rows(nc.gpsimd, F32, planes, scales, a, quadrant)
 
         x_pairs = x_sb[:].bitcast(F32)
         x_codes = keep.tile([P, GROUPS * P], U32, name="x_codes", align_bytes=64)

@@ -81,15 +81,15 @@ def tile_attention_pa_k_kernel(
         k_planes = zeroed_planes(KV_COLS, "k")
         v_planes = zeroed_planes(KV_COLS, "v")
 
-        def load_scale_rows(queue, view, planes, scales, a, quadrant):
+        def load_scale_rows(planes, scales, a, quadrant):
             first = 32 * quadrant
-            queue.dma_start(
-                out=planes[first : first + PLANES_TOGETHER * ROWS_PER_QUADRANT, a, :].bitcast(view),
+            nc.gpsimd.dma_start(
+                out=planes[first : first + PLANES_TOGETHER * ROWS_PER_QUADRANT, a, :].bitcast(F32),
                 in_=scales[
                     PLANES_TOGETHER * a : PLANES_TOGETHER * (a + 1),
                     ROWS_PER_QUADRANT * quadrant : ROWS_PER_QUADRANT * (quadrant + 1),
                     :,
-                ].bitcast(view),
+                ].bitcast(F32),
             )
 
         x_rows = x.rearrange("b t c -> (b t) c")
@@ -97,18 +97,11 @@ def tile_attention_pa_k_kernel(
         for chunk in range(X_CHUNKS):
             cols = slice(chunk * X_CHUNK_GROUPS * K_PASS, (chunk + 1) * X_CHUNK_GROUPS * K_PASS)
             nc.sync.dma_start(out=x_sb[:, cols], in_=x_rows[:, cols])
-            for quadrant in range(2):
-                load_scale_rows(nc.sync, I32, q_planes, q_kernel_scales, chunk, quadrant)
         q_words = []
         for g in range(GROUPS):
             tile_q = weights.tile([P, Q_COLS], U32, name="tile_q", tag="words", align_bytes=64)
             nc.sync.dma_start(out=tile_q[:].bitcast(I32), in_=words_of_group(q_kernel_words, g))
             q_words.append(tile_q)
-            a, quadrant = divmod(g % (2 * ROUNDS), 2)
-            if g < 2 * ROUNDS:
-                load_scale_rows(nc.sync, I32, k_planes, k_kernel_scales, a, quadrant)
-            else:
-                load_scale_rows(nc.sync, I32, v_planes, v_kernel_scales, a, quadrant)
 
         identity = keep.tile([P, P], F32, name="identity")
         make_identity(nc, identity[:])
@@ -120,8 +113,8 @@ def tile_attention_pa_k_kernel(
             (v_planes, v_kernel_scales),
         ):
             for a in range(ROUNDS):
-                for quadrant in range(2, QUADRANTS):
-                    load_scale_rows(nc.gpsimd, F32, planes, scales, a, quadrant)
+                for quadrant in range(QUADRANTS):
+                    load_scale_rows(planes, scales, a, quadrant)
 
         x_pairs = x_sb[:].bitcast(F32)
         x_codes = keep.tile([P, GROUPS * P], U32, name="x_codes", align_bytes=64)

@@ -64,7 +64,6 @@ def tile_attention_pa_k_kernel(
         keep = ctx.enter_context(tc.tile_pool(name="keep", bufs=1))
         weights = ctx.enter_context(tc.tile_pool(name="weights", bufs=GROUPS))
         stage = ctx.enter_context(tc.tile_pool(name="stage", bufs=2))
-        results = ctx.enter_context(tc.tile_pool(name="results", bufs=Q_COLS // BANK + 1))
         psum_x = ctx.enter_context(tc.psum_pool(name="psum_x", bufs=2))
         psum_acc = ctx.enter_context(tc.psum_pool(name="psum_acc", bufs=1))
         ctx.enter_context(tc.manual_schedule())
@@ -94,9 +93,7 @@ def tile_attention_pa_k_kernel(
 
         x_rows = x.rearrange("b t c -> (b t) c")
         x_sb = keep.tile([P, C], BF16, name="x_sb")
-        for chunk in range(X_CHUNKS):
-            cols = slice(chunk * X_CHUNK_GROUPS * K_PASS, (chunk + 1) * X_CHUNK_GROUPS * K_PASS)
-            nc.sync.dma_start(out=x_sb[:, cols], in_=x_rows[:, cols])
+        nc.sync.dma_start(out=x_sb[:], in_=x_rows)
         q_words = []
         for g in range(GROUPS):
             tile_q = weights.tile([P, Q_COLS], U32, name="tile_q", tag="words", align_bytes=64)
@@ -220,13 +217,13 @@ def tile_attention_pa_k_kernel(
                 stop=(g == GROUPS - 1),
             )
 
-        def rotate_and_store(acc, tables, dest):
+        def rotate(acc, tables, result):
             cos_tab, sin_tab = tables
             heads = acc[:].rearrange("p (h d) -> p h d", d=HEAD_DIM)
             shape = [P, HEADS_PER_BANK, HEAD_DIM]
             by_cos = stage.tile([P, HEADS_PER_BANK, 2, HALF], F32, name="by_cos")
             by_sin = stage.tile([P, HEADS_PER_BANK, 2, HALF], F32, name="by_sin")
-            rotated = results.tile([P, HEADS_PER_BANK, 2, HALF], F32, name="rotated")
+            rotated = result.rearrange("p (h s f) -> p h s f", s=2, f=HALF)
             nc.vector.tensor_tensor(
                 out=by_cos[:].rearrange("p h s f -> p h (s f)"),
                 in0=heads,
@@ -246,7 +243,6 @@ def tile_attention_pa_k_kernel(
                     in1=by_sin[:, :, 1 - half, :],
                     op=ALU.add,
                 )
-            nc.sync.dma_start(out=dest, in_=rotated[:].rearrange("p h s f -> p (h s f)"))
 
         q_banks = Q_COLS // BANK
         acc_q = [psum_acc.tile([P, BANK], F32, name="acc_q%d" % bank) for bank in range(q_banks)]
@@ -267,15 +263,18 @@ def tile_attention_pa_k_kernel(
                     )
                 kv_words.append(tile_kv)
 
-        q_out = out_0.rearrange("b t k g d -> (b t) (k g d)")
+        q_rotated = keep.tile([P, Q_COLS], F32, name="q_rotated")
         for bank in range(q_banks):
-            rotate_and_store(acc_q[bank], q_tables, q_out[:, bank * BANK : (bank + 1) * BANK])
+            rotate(acc_q[bank], q_tables, q_rotated[:, bank * BANK : (bank + 1) * BANK])
+        nc.sync.dma_start(out=out_0.rearrange("b t k g d -> (b t) (k g d)"), in_=q_rotated[:])
 
         acc_k = psum_acc.tile([P, BANK], F32, name="acc_k")
         for g in range(GROUPS):
             a, j = divmod(g, PLANES_TOGETHER)
             mx_pass(acc_k, g, kv_words[a][:, j, :], k_planes, 0)
-        rotate_and_store(acc_k, k_tables, out_1.rearrange("b t k d -> (b t) (k d)"))
+        k_rotated = keep.tile([P, KV_COLS], F32, name="k_rotated")
+        rotate(acc_k, k_tables, k_rotated[:])
+        nc.sync.dma_start(out=out_1.rearrange("b t k d -> (b t) (k d)"), in_=k_rotated[:])
 
         acc_v = psum_acc.tile([P, BANK], F32, name="acc_v")
         for g in range(GROUPS):

@@ -80,15 +80,15 @@ def tile_attention_pa_k_kernel(
         k_planes = zeroed_planes(KV_COLS, "k")
         v_planes = zeroed_planes(KV_COLS, "v")
 
-        def load_scale_rows(planes, scales, a, quadrant):
+        def load_scale_rows(queue, view, planes, scales, a, quadrant):
             first = 32 * quadrant
-            nc.gpsimd.dma_start(
-                out=planes[first : first + PLANES_TOGETHER * ROWS_PER_QUADRANT, a, :].bitcast(F32),
+            queue.dma_start(
+                out=planes[first : first + PLANES_TOGETHER * ROWS_PER_QUADRANT, a, :].bitcast(view),
                 in_=scales[
                     PLANES_TOGETHER * a : PLANES_TOGETHER * (a + 1),
                     ROWS_PER_QUADRANT * quadrant : ROWS_PER_QUADRANT * (quadrant + 1),
                     :,
-                ].bitcast(F32),
+                ].bitcast(view),
             )
 
         x_rows = x.rearrange("b t c -> (b t) c")
@@ -99,6 +99,7 @@ def tile_attention_pa_k_kernel(
             tile_q = weights.tile([P, Q_COLS], U32, name="tile_q", tag="words", align_bytes=64)
             nc.sync.dma_start(out=tile_q[:].bitcast(I32), in_=words_of_group(q_kernel_words, g))
             q_words.append(tile_q)
+            load_scale_rows(nc.sync, I32, v_planes, v_kernel_scales, *divmod(g, QUADRANTS))
 
         identity = keep.tile([P, P], F32, name="identity")
         make_identity(nc, identity[:])
@@ -107,11 +108,10 @@ def tile_attention_pa_k_kernel(
         for planes, scales in (
             (q_planes, q_kernel_scales),
             (k_planes, k_kernel_scales),
-            (v_planes, v_kernel_scales),
         ):
             for a in range(ROUNDS):
                 for quadrant in range(QUADRANTS):
-                    load_scale_rows(planes, scales, a, quadrant)
+                    load_scale_rows(nc.gpsimd, F32, planes, scales, a, quadrant)
 
         x_pairs = x_sb[:].bitcast(F32)
         x_codes = keep.tile([P, GROUPS * P], U32, name="x_codes", align_bytes=64)

import math
from contextlib import ExitStack

import concourse.mybir as mybir
from concourse.masks import make_identity

F32 = mybir.dt.float32
BF16 = mybir.dt.bfloat16
I32 = mybir.dt.int32
U32 = mybir.dt.uint32
U8 = mybir.dt.uint8
FP8X4 = mybir.dt.float8_e4m3fn_x4
ALU = mybir.AluOpType
ACT = mybir.ActivationFunctionType

P = 128
PACK = 4
K_PASS = P * PACK
C = 8192
GROUPS = C // K_PASS
POSITIONS = 64
HEAD_DIM = 128
HALF = HEAD_DIM // 2
BANK = 512
HEADS_PER_BANK = BANK // HEAD_DIM
Q_COLS = 2048
KV_COLS = 512
ALL_COLS = Q_COLS + 2 * KV_COLS

PLANES_TOGETHER = 4
ROUNDS = GROUPS // PLANES_TOGETHER
QUADRANTS = 4
ROWS_PER_QUADRANT = 4

X_CHUNK_GROUPS = 4
X_CHUNKS = GROUPS // X_CHUNK_GROUPS
WORDS_PER_GROUP = K_PASS // 2

ROPE_THETA = 10000.0
FREQ_RATIO = ROPE_THETA ** (-1.0 / HALF)
TWO_PI = 2.0 * math.pi
TWO_PI_HIGH = 6.28125
TWO_PI_LOW = TWO_PI - TWO_PI_HIGH
ROUND_MAGIC = 1.5 * 2.0**23

FLOPS = 2 * P * C * ALL_COLS


def tile_attention_pa_k_kernel(
    tc,
    x,
    q_kernel_words,
    q_kernel_scales,
    k_kernel_words,
    k_kernel_scales,
    v_kernel_words,
    v_kernel_scales,
    out_0,
    out_1,
    out_2,
):
    nc = tc.nc
    with ExitStack() as ctx:
        keep = ctx.enter_context(tc.tile_pool(name="keep", bufs=1))
        weights = ctx.enter_context(tc.tile_pool(name="weights", bufs=GROUPS))
        stage = ctx.enter_context(tc.tile_pool(name="stage", bufs=2))
        psum_x = ctx.enter_context(tc.psum_pool(name="psum_x", bufs=2))
        psum_acc = ctx.enter_context(tc.psum_pool(name="psum_acc", bufs=1))
        ctx.enter_context(tc.manual_schedule())

        def words_of_group(words, g):
            return words[g].rearrange("p n t -> p (n t)").bitcast(I32)

        def zeroed_planes(width, label):
            planes = keep.tile([P, ROUNDS, width], U8, name="planes_" + label, align_bytes=64)
            nc.vector.memset(planes[:].bitcast(I32), 0)
            return planes

        q_planes = zeroed_planes(Q_COLS, "q")
        k_planes = zeroed_planes(KV_COLS, "k")
        v_planes = zeroed_planes(KV_COLS, "v")

        def load_scale_rows(queue, view, planes, scales, a, quadrant):
            first = 32 * quadrant
            queue.dma_start(
                out=planes[first : first + PLANES_TOGETHER * ROWS_PER_QUADRANT, a, :].bitcast(view),
                in_=scales[
                    PLANES_TOGETHER * a : PLANES_TOGETHER * (a + 1),
                    ROWS_PER_QUADRANT * quadrant : ROWS_PER_QUADRANT * (quadrant + 1),
                    :,
                ].bitcast(view),
            )

        x_rows = x.rearrange("b t c -> (b t) c")
        x_sb = keep.tile([P, C], BF16, name="x_sb")
        nc.sync.dma_start(out=x_sb[:], in_=x_rows)
        q_words = []
        for g in range(GROUPS):
            tile_q = weights.tile([P, Q_COLS], U32, name="tile_q", tag="words", align_bytes=64)
            nc.sync.dma_start(out=tile_q[:].bitcast(I32), in_=words_of_group(q_kernel_words, g))
            q_words.append(tile_q)
            load_scale_rows(nc.sync, I32, v_planes, v_kernel_scales, *divmod(g, QUADRANTS))

        identity = keep.tile([P, P], F32, name="identity")
        make_identity(nc, identity[:])
        row_number = keep.tile([P, 1], I32, name="row_number")
        nc.gpsimd.iota(row_number[:], pattern=[[0, 1]], base=0, channel_multiplier=1)
        for planes, scales in (
            (q_planes, q_kernel_scales),
            (k_planes, k_kernel_scales),
        ):
            for a in range(ROUNDS):
                for quadrant in range(QUADRANTS):
                    load_scale_rows(nc.gpsimd, F32, planes, scales, a, quadrant)

        x_pairs = x_sb[:].bitcast(F32)
        x_codes = keep.tile([P, GROUPS * P], U32, name="x_codes", align_bytes=64)
        x_scales = keep.tile([P, GROUPS * P], U8, name="x_scales", align_bytes=64)
        for chunk in range(X_CHUNKS):
            grouped = stage.tile([P, X_CHUNK_GROUPS, P, PACK], BF16, name="grouped", align_bytes=64)
            for pair in range(X_CHUNK_GROUPS // 2):
                turned = psum_x.tile([P, 2, 2, P], F32, name="turned")
                for i in range(2):
                    first = (chunk * X_CHUNK_GROUPS + 2 * pair + i) * WORDS_PER_GROUP
                    for u in range(2):
                        nc.tensor.transpose(
                            turned[:, i, u, :],
                            x_pairs[:, first + u : first + WORDS_PER_GROUP : 2],
                            identity[:],
                        )
                nc.scalar.copy(
                    out=grouped[:, 2 * pair : 2 * pair + 2, :, :].bitcast(F32),
                    in_=turned[:].rearrange("p i u r -> p i r u"),
                )
            cols = slice(chunk * X_CHUNK_GROUPS * P, (chunk + 1) * X_CHUNK_GROUPS * P)
            nc.vector.quantize_mx(
                out=x_codes[:, cols].bitcast(FP8X4),
                scales=x_scales[:, cols],
                in_=grouped[:].rearrange("p g r t -> p (g r t)"),
            )

        position_int = keep.tile([P, 1], I32, name="position_int")
        nc.vector.tensor_scalar(
            out=position_int[:], in0=row_number[:], scalar1=POSITIONS - 1, scalar2=None, op0=ALU.bitwise_and
        )
        position = keep.tile([P, 1], F32, name="position")
        nc.vector.tensor_copy(out=position[:], in_=position_int[:])
        inv_freq = keep.tile([P, HALF], F32, name="inv_freq")
        nc.vector.memset(inv_freq[:, 0:1], 1.0)
        for doubling in range(6):
            done = 1 << doubling
            nc.vector.tensor_scalar(
                out=inv_freq[:, done : 2 * done],
                in0=inv_freq[:, 0:done],
                scalar1=FREQ_RATIO**done,
                scalar2=None,
                op0=ALU.mult,
            )
        angle = keep.tile([P, 2, HALF], F32, name="angle")
        nc.vector.tensor_scalar(
            out=angle[:, 0, :], in0=inv_freq[:], scalar1=position[:, 0:1], scalar2=None, op0=ALU.mult
        )
        nc.vector.tensor_scalar(
            out=angle[:, 1, :],
            in0=inv_freq[:],
            scalar1=position[:, 0:1],
            scalar2=math.pi / 2.0,
            op0=ALU.mult,
            op1=ALU.add,
        )
        turns = keep.tile([P, 2, HALF], F32, name="turns")
        nc.vector.tensor_scalar(
            out=turns[:], in0=angle[:], scalar1=1.0 / TWO_PI, scalar2=ROUND_MAGIC, op0=ALU.mult, op1=ALU.add
        )
        nc.vector.tensor_scalar(out=turns[:], in0=turns[:], scalar1=ROUND_MAGIC, scalar2=None, op0=ALU.subtract)
        reduced = keep.tile([P, 2, HALF], F32, name="reduced")
        nc.vector.scalar_tensor_tensor(
            out=reduced[:], in0=turns[:], scalar=-TWO_PI_HIGH, in1=angle[:], op0=ALU.mult, op1=ALU.add
        )
        nc.vector.scalar_tensor_tensor(
            out=reduced[:], in0=turns[:], scalar=-TWO_PI_LOW, in1=reduced[:], op0=ALU.mult, op1=ALU.add
        )
        sin_cos = keep.tile([P, 2, HALF], F32, name="sin_cos")
        nc.scalar.activation(out=sin_cos[:], in_=reduced[:], func=ACT.Sin)

        def rotation_tables(factor, label):
            cos_tab = keep.tile([P, 2, HALF], F32, name="cos_" + label)
            sin_tab = keep.tile([P, 2, HALF], F32, name="sin_" + label)
            nc.vector.tensor_scalar(
                out=cos_tab[:],
                in0=sin_cos[:, 1:2, :].to_broadcast([P, 2, HALF]),
                scalar1=factor,
                scalar2=None,
                op0=ALU.mult,
            )
            nc.vector.tensor_scalar(
                out=sin_tab[:, 0, :], in0=sin_cos[:, 0, :], scalar1=factor, scalar2=None, op0=ALU.mult
            )
            nc.vector.tensor_scalar(
                out=sin_tab[:, 1, :], in0=sin_cos[:, 0, :], scalar1=-factor, scalar2=None, op0=ALU.mult
            )
            return cos_tab, sin_tab

        q_tables = rotation_tables(HEAD_DIM**-0.5, "q")
        k_tables = rotation_tables(1.0, "k")

        def mx_pass(acc, g, words, planes, plane_start):
            a, j = divmod(g, PLANES_TOGETHER)
            tokens = slice(g * P, (g + 1) * P)
            nc.tensor.matmul_mx(
                out=acc[:],
                lhsT=x_codes[:, tokens].bitcast(FP8X4),
                lhsT_scale=x_scales[:, tokens],
                rhs=words.bitcast(FP8X4),
                rhs_scale=planes[ROWS_PER_QUADRANT * j : P, a, plane_start : plane_start + BANK],
                start=(g == 0),
                stop=(g == GROUPS - 1),
            )

        def rotate(acc, tables, result):
            cos_tab, sin_tab = tables
            heads = acc[:].rearrange("p (h d) -> p h d", d=HEAD_DIM)
            shape = [P, HEADS_PER_BANK, HEAD_DIM]
            by_cos = stage.tile([P, HEADS_PER_BANK, 2, HALF], F32, name="by_cos")
            by_sin = stage.tile([P, HEADS_PER_BANK, 2, HALF], F32, name="by_sin")
            rotated = result.rearrange("p (h s f) -> p h s f", s=2, f=HALF)
            nc.vector.tensor_tensor(
                out=by_cos[:].rearrange("p h s f -> p h (s f)"),
                in0=heads,
                in1=cos_tab[:].rearrange("p s f -> p (s f)").unsqueeze(1).to_broadcast(shape),
                op=ALU.mult,
            )
            nc.vector.tensor_tensor(
                out=by_sin[:].rearrange("p h s f -> p h (s f)"),
                in0=heads,
                in1=sin_tab[:].rearrange("p s f -> p (s f)").unsqueeze(1).to_broadcast(shape),
                op=ALU.mult,
            )
            for half in range(2):
                nc.vector.tensor_tensor(
                    out=rotated[:, :, half, :],
                    in0=by_cos[:, :, half, :],
                    in1=by_sin[:, :, 1 - half, :],
                    op=ALU.add,
                )

        q_banks = Q_COLS // BANK
        acc_q = [psum_acc.tile([P, BANK], F32, name="acc_q%d" % bank) for bank in range(q_banks)]
        for g in range(GROUPS):
            for bank in range(q_banks):
                mx_pass(acc_q[bank], g, q_words[g][:, bank * BANK : (bank + 1) * BANK], q_planes, bank * BANK)

        kv_words = []
        for words in (k_kernel_words, v_kernel_words):
            for a in range(ROUNDS):
                tile_kv = weights.tile(
                    [P, PLANES_TOGETHER, KV_COLS], U32, name="tile_kv", tag="words", align_bytes=64
                )
                for j in range(PLANES_TOGETHER):
                    nc.sync.dma_start(
                        out=tile_kv[:, j, :].bitcast(I32),
                        in_=words_of_group(words, PLANES_TOGETHER * a + j),
                    )
                kv_words.append(tile_kv)

        q_rotated = keep.tile([P, Q_COLS], F32, name="q_rotated")
        for bank in range(q_banks):
            rotate(acc_q[bank], q_tables, q_rotated[:, bank * BANK : (bank + 1) * BANK])
        nc.sync.dma_start(out=out_0.rearrange("b t k g d -> (b t) (k g d)"), in_=q_rotated[:])

        acc_k = psum_acc.tile([P, BANK], F32, name="acc_k")
        for g in range(GROUPS):
            a, j = divmod(g, PLANES_TOGETHER)
            mx_pass(acc_k, g, kv_words[a][:, j, :], k_planes, 0)
        k_rotated = keep.tile([P, KV_COLS], F32, name="k_rotated")
        rotate(acc_k, k_tables, k_rotated[:])
        nc.sync.dma_start(out=out_1.rearrange("b t k d -> (b t) (k d)"), in_=k_rotated[:])

        acc_v = psum_acc.tile([P, BANK], F32, name="acc_v")
        for g in range(GROUPS):
            a, j = divmod(g, PLANES_TOGETHER)
            mx_pass(acc_v, g, kv_words[ROUNDS + a][:, j, :], v_planes, 0)
        v_sb = stage.tile([P, BANK], F32, name="v_sb")
        nc.vector.tensor_copy(out=v_sb[:], in_=acc_v[:])
        nc.sync.dma_start(out=out_2.rearrange("b t k d -> (b t) (k d)"), in_=v_sb[:])
